import numpy as np
import ml_dtypes


def mxq(x, axis, fmt="e4m3"):
    dtype, down = {"e4m3": (ml_dtypes.float8_e4m3fn, 7), "e5m2": (ml_dtypes.float8_e5m2, 14)}[fmt]
    v = np.moveaxis(np.asarray(x, np.float32).astype(ml_dtypes.bfloat16).astype(np.float64), axis, -1)
    blocks = v.reshape(v.shape[:-1] + (-1, 32))
    amax = np.abs(blocks).max(-1, keepdims=True)
    byte = np.maximum(np.where(amax > 0, np.frexp(amax)[1] - 1 + 127, 0) - down, 1)
    scale = np.exp2(byte - 127.0)
    codes = (blocks / scale).astype(np.float32).astype(dtype).astype(np.float64)
    return np.moveaxis((codes * scale).reshape(v.shape), -1, axis)


WIDE = False


def mx_kscale(k):
    if not WIDE:
        return np.ones(k)
    levels = np.array([20, -20, 10, -10, 0])
    a = np.random.permutation(np.resize(levels, k // 512 * 4)).reshape(k // 512, 4)
    idx = np.arange(k)
    return np.exp2(a[idx // 512, idx % 128 // 32])


BF16 = ml_dtypes.bfloat16


def bf(x):
    return np.asarray(x, np.float32).astype(BF16)


def f64(x):
    return np.asarray(x).astype(np.float64)


B, CIN, COUT, H, W, NOFF, PAD = 64, 256, 512, 8, 9, 9, 4
BH = B * H


def tokens(a):
    return np.ascontiguousarray(a.transpose(3, 0, 2, 1)).reshape(-1, a.shape[1])


def span(i):
    d = i - PAD
    return d, max(0, -d), W - max(0, d)


def setup_inputs():
    s = mx_kscale(W * BH).reshape(W, B, H).transpose(1, 2, 0)[:, None, :, :]
    inp = {}
    for i in range(NOFF):
        d, lo, hi = span(i)
        f = np.ones((B, 1, H, W))
        f[:, :, :, lo:hi] = s[:, :, :, lo + d:hi + d]
        inp["x%d" % i] = bf(np.random.standard_normal((B, CIN, H, W)) * f)
    inp["weights"] = bf(np.random.standard_normal((NOFF, COUT, CIN)) * 0.6 / np.sqrt(CIN))
    inp["bias"] = bf(np.random.standard_normal((NOFF, COUT)) * 0.4)
    g = np.random.standard_normal((B, COUT, H, W)) * np.exp2(np.random.randint(-12, 1, (B, 1, H, W))) / s
    inp["grad_out"] = bf(g)
    return inp


def reference(x0, x1, x2, x3, x4, x5, x6, x7, x8, weights, bias, grad_out):
    xs = [x0, x1, x2, x3, x4, x5, x6, x7, x8]
    gq = mxq(tokens(f64(grad_out)), 0, "e5m2")
    out = np.zeros((NOFF, COUT, CIN))
    for i in range(NOFF):
        d, lo, hi = span(i)
        xq = mxq(tokens(f64(xs[i])[:, :, :, lo:hi]), 0, "e4m3")
        out[i] = gq[(lo + d) * BH:(hi + d) * BH].T @ xq
    return out

@@ -1,0 +1,173 @@
+from contextlib import ExitStack
+
+import concourse.mybir as mybir
+
+BF16 = mybir.dt.bfloat16
+F32 = mybir.dt.float32
+U32 = mybir.dt.uint32
+U8 = mybir.dt.uint8
+I32 = mybir.dt.int32
+E4X4 = mybir.dt.float8_e4m3fn_x4
+E5X4 = mybir.dt.float8_e5m2_x4
+
+P = 128
+W = 9
+PADW = 4
+HW = 72
+HALF = 36
+ROW = 128 * HW
+FLOPS = 2 * 61 * 512 * 512 * 256
+
+
+def span(i):
+    d = i - PADW
+    return d, max(0, -d), W - max(0, d)
+
+
+def tile_scatterhorizontal_kernel(tc, x0, x1, x2, x3, x4, x5, x6, x7, x8, weights, bias, grad_out, out):
+    nc = tc.nc
+    xs = [x0, x1, x2, x3, x4, x5, x6, x7, x8]
+    pairs = [(0, 1), (2, 3), (4, 5), (6, 7), (8,)]
+    with ExitStack() as ctx:
+        keep = ctx.enter_context(tc.tile_pool(name="keep", bufs=1))
+        psum = ctx.enter_context(tc.psum_pool(name="psum", bufs=8))
+        ctx.enter_context(tc.manual_schedule())
+
+        raws = []
+        bts = []
+        qs = []
+        for j in range(3):
+            cols = W if j < 2 else W - 1
+            raw_t = keep.tile([P, 129 * HW], BF16, name="raw%d" % j)
+            bt_t = keep.tile([P, cols, 129, 4], BF16, name="bt%d" % j)
+            q_t = keep.tile([P, cols, 2, 128, 4], BF16, name="q%d" % j, align_bytes=64)
+            nc.vector.memset(raw_t[:, 0:48], 0.0)
+            nc.vector.memset(raw_t[:, ROW:ROW + HW], 0.0)
+            raws.append(raw_t)
+            bts.append(bt_t)
+            qs.append(q_t)
+        xcs = []
+        xss = []
+        for j in range(2):
+            xc_t = keep.tile([P, W - j, 512], U32, name="xc%d" % j, align_bytes=64)
+            xs_t = keep.tile([P, W - j, 512], U8, name="xs%d" % j, align_bytes=64)
+            xcs.append(xc_t)
+            xss.append(xs_t)
+        gc = keep.tile([P, W, 512], U32, name="gc", align_bytes=64)
+        gs = keep.tile([P, W, 512], U8, name="gs", align_bytes=64)
+        osts = []
+        for j in range(4):
+            ost_t = keep.tile([P, 4, 512], F32, name="ost%d" % j)
+            osts.append(ost_t)
+        osts.append(osts[0])
+
+        units = []
+        for half in range(2):
+            units.append((grad_out, 256 * half, 0, W, E5X4, gc, gs, 0, 256 * half))
+        bounds = []
+        for pi, pair in enumerate(pairs):
+            c0 = min(span(i)[1] + span(i)[0] for i in pair)
+            c1 = max(span(i)[2] + span(i)[0] for i in pair)
+            bounds.append((c0, c1))
+            for j, i in enumerate(pair):
+                d, lo, hi = span(i)
+                units.append((xs[i], 0, lo, hi, E4X4, xcs[pi % 2], xss[pi % 2], d - c0, 256 * j))
+        n_units = len(units)
+        first_unit = [2 + 2 * pi for pi in range(5)]
+        last_unit = [3, 5, 7, 9, 10]
+
+        def load(u):
+            src, cb = units[u][0], units[u][1]
+            raw = raws[u % 3]
+            flat = src.rearrange("b k h w -> b (k h w)")
+            nc.sync.dma_start(out=raw[0:P:2, HALF:HALF + ROW], in_=flat[:, cb * HW:cb * HW + ROW])
+            nc.sync.dma_start(out=raw[1:P:2, 0:ROW], in_=flat[:, (cb + 128) * HW:(cb + 128) * HW + ROW])
+
+        def regroup(u):
+            lo, hi = units[u][2], units[u][3]
+            n = hi - lo
+            raw = raws[u % 3]
+            bt = bts[u % 3]
+            q = qs[u % 3]
+            a_view = raw[:, HALF:HALF + ROW].rearrange("p (k g t w) -> p g w k t", g=2, t=4, w=W)
+            b_view = raw[:, 0:129 * HW].rearrange("p (k g t w) -> p g w k t", g=2, t=4, w=W)
+            nc.vector.tensor_copy(out=q[:, 0:n, 0, :, :], in_=a_view[:, 0, lo:hi, :, :])
+            nc.scalar.copy(out=bt[:, 0:n, :, :], in_=b_view[:, 0, lo:hi, :, :])
+            nc.vector.tensor_copy(out=q[:, 0:n, 1, :, :], in_=q[:, 0:n, 0, :, :])
+            nc.scalar.dma_start(out=q[1:P:2, 0:n, 0, :, :], in_=bt[0:P:2, 0:n, 1:129, :])
+            nc.scalar.dma_start(out=q[0:P:2, 0:n, 1, :, :], in_=bt[1:P:2, 0:n, 0:128, :])
+
+        def zero_slots(pi):
+            c0, c1 = bounds[pi]
+            for j, i in enumerate(pairs[pi]):
+                d, lo, hi = span(i)
+                for cp in range(c0, c1):
+                    if cp < lo + d or cp >= hi + d:
+                        nc.vector.memset(xcs[pi % 2][:, cp - c0, 256 * j:256 * j + 256].bitcast(I32), 0)
+                        nc.vector.memset(xss[pi % 2][:, cp - c0, 256 * j:256 * j + 256].bitcast(I32), 0)
+
+        def quantise(u):
+            lo, hi, fmt, codes, scales, shift, off = units[u][2:9]
+            q = qs[u % 3]
+            for ci in range(hi - lo):
+                slot = lo + ci + shift
+                nc.vector.quantize_mx(
+                    out=codes[:, slot, off:off + 256].bitcast(fmt),
+                    scales=scales[:, slot, off:off + 256],
+                    in_=q[:, ci, :, :, :].rearrange("p s k t -> p (s k t)"),
+                )
+
+        accs = {}
+
+        def matmuls(pi):
+            c0, c1 = bounds[pi]
+            for ot in range(4):
+                acc = psum.tile([P, 512], F32, tag="acc")
+                accs[(pi, ot)] = acc
+            for cp in range(c0, c1):
+                for ot in range(4):
+                    nc.tensor.matmul_mx(
+                        out=accs[(pi, ot)][:],
+                        lhsT=gc[:, cp, 128 * ot:128 * ot + 128].bitcast(E5X4),
+                        lhsT_scale=gs[:, cp, 128 * ot:128 * ot + 128],
+                        rhs=xcs[pi % 2][:, cp - c0, :].bitcast(E4X4),
+                        rhs_scale=xss[pi % 2][:, cp - c0, :],
+                        start=(cp == c0),
+                        stop=(cp == c1 - 1),
+                    )
+
+        def evac(pi):
+            width = 256 * len(pairs[pi])
+            for ot in range(4):
+                nc.scalar.copy(out=osts[pi][:, ot, 0:width], in_=accs[(pi, ot)][:, 0:width])
+
+        def store(pi):
+            for j, i in enumerate(pairs[pi]):
+                nc.sync.dma_start(
+                    out=out[i].rearrange("(t o) k -> o t k", o=P),
+                    in_=osts[pi][:, :, 256 * j:256 * j + 256],
+                )
+
+        waiting = []
+        for t in range(n_units + 5):
+            if t == 0:
+                load(0)
+                load(1)
+            if t + 2 < n_units:
+                load(t + 2)
+            if t < n_units:
+                regroup(t)
+            z = t - 2
+            if 0 <= z < n_units:
+                if z in first_unit:
+                    zero_slots(first_unit.index(z))
+                quantise(z)
+                if z in last_unit:
+                    matmuls(last_unit.index(z))
+            if t - 4 in last_unit:
+                evac(last_unit.index(t - 4))
+                waiting.append(last_unit.index(t - 4))
+            if t + 2 >= n_units - 1:
+                for pi in waiting:
+                    store(pi)
+                waiting = []

@@ -89,10 +89,20 @@ def tile_scatterhorizontal_kernel(tc, x0, x1, x2, x3, x4, x5, x6, x7, x8, weight
             raw = raws[u % 3]
             bt = bts[u % 3]
             q = qs[u % 3]
-            a_view = raw[:, HALF:HALF + ROW].rearrange("p (k g t w) -> p g w k t", g=2, t=4, w=W)
-            b_view = raw[:, 0:129 * HW].rearrange("p (k g t w) -> p g w k t", g=2, t=4, w=W)
-            nc.vector.tensor_copy(out=q[:, 0:n, 0, :, :], in_=a_view[:, 0, lo:hi, :, :])
-            nc.scalar.copy(out=bt[:, 0:n, :, :], in_=b_view[:, 0, lo:hi, :, :])
+            a_view = raw[:, HALF:HALF + ROW].rearrange("p (k g t w) -> p g k t w", g=2, t=4, w=W)
+            b_view = raw[:, 0:129 * HW].rearrange("p (k g t w) -> p g k t w", g=2, t=4, w=W)
+            parts = (n + 3) // 4
+            cuts = [(n * j) // parts for j in range(parts + 1)]
+            for j in range(parts):
+                e0, e1 = cuts[j], cuts[j + 1]
+                nc.vector.tensor_copy(
+                    out=q[:, e0:e1, 0, :, :].rearrange("p c k t -> p k t c"),
+                    in_=a_view[:, 0, :, :, lo + e0:lo + e1],
+                )
+                nc.scalar.copy(
+                    out=bt[:, e0:e1, :, :].rearrange("p c k t -> p k t c"),
+                    in_=b_view[:, 0, :, :, lo + e0:lo + e1],
+                )
             nc.vector.tensor_copy(out=q[:, 0:n, 1, :, :], in_=q[:, 0:n, 0, :, :])
             nc.scalar.dma_start(out=q[1:P:2, 0:n, 0, :, :], in_=bt[0:P:2, 0:n, 1:129, :])
             nc.scalar.dma_start(out=q[0:P:2, 0:n, 1, :, :], in_=bt[1:P:2, 0:n, 0:128, :])

@@ -16,6 +16,7 @@ PADW = 4
 HW = 72
 HALF = 36
 ROW = 128 * HW
+PITCH = 136
 FLOPS = 2 * 61 * 512 * 512 * 256
 
 
@@ -27,7 +28,7 @@ def span(i):
 def tile_scatterhorizontal_kernel(tc, x0, x1, x2, x3, x4, x5, x6, x7, x8, weights, bias, grad_out, out):
     nc = tc.nc
     xs = [x0, x1, x2, x3, x4, x5, x6, x7, x8]
-    pairs = [(0, 1), (2, 3), (4, 5), (6, 7), (8,)]
+    pairs = [(0,), (1, 2), (3, 4), (5, 6), (7, 8)]
     with ExitStack() as ctx:
         keep = ctx.enter_context(tc.tile_pool(name="keep", bufs=1))
         psum = ctx.enter_context(tc.psum_pool(name="psum", bufs=8))
@@ -39,13 +40,16 @@ def tile_scatterhorizontal_kernel(tc, x0, x1, x2, x3, x4, x5, x6, x7, x8, weight
         for j in range(3):
             cols = W if j < 2 else W - 1
             raw_t = keep.tile([P, 129 * HW], BF16, name="raw%d" % j)
-            bt_t = keep.tile([P, cols, 129, 4], BF16, name="bt%d" % j)
-            q_t = keep.tile([P, cols, 2, 128, 4], BF16, name="q%d" % j, align_bytes=64)
+            bt_t = keep.tile([P, cols, PITCH, 4], BF16, name="bt%d" % j)
+            qa_t = keep.tile([P, cols, PITCH, 4], BF16, name="qa%d" % j, align_bytes=64)
+            qb_t = keep.tile([P, cols, PITCH, 4], BF16, name="qb%d" % j, align_bytes=64)
             nc.vector.memset(raw_t[:, 0:48], 0.0)
             nc.vector.memset(raw_t[:, ROW:ROW + HW], 0.0)
+            nc.vector.memset(bt_t[:, :, 128:PITCH, :], 0.0)
+            nc.vector.memset(qa_t[:, :, 128:PITCH, :], 0.0)
             raws.append(raw_t)
             bts.append(bt_t)
-            qs.append(q_t)
+            qs.append((qa_t, qb_t))
         xcs = []
         xss = []
         for j in range(2):
@@ -59,22 +63,24 @@ def tile_scatterhorizontal_kernel(tc, x0, x1, x2, x3, x4, x5, x6, x7, x8, weight
         for j in range(4):
             ost_t = keep.tile([P, 4, 512], F32, name="ost%d" % j)
             osts.append(ost_t)
-        osts.append(osts[0])
+        osts = [osts[3]] + osts
 
         units = []
         for half in range(2):
             units.append((grad_out, 256 * half, 0, W, E5X4, gc, gs, 0, 256 * half))
         bounds = []
+        first_unit = []
+        last_unit = []
         for pi, pair in enumerate(pairs):
             c0 = min(span(i)[1] + span(i)[0] for i in pair)
             c1 = max(span(i)[2] + span(i)[0] for i in pair)
             bounds.append((c0, c1))
+            first_unit.append(len(units))
             for j, i in enumerate(pair):
                 d, lo, hi = span(i)
                 units.append((xs[i], 0, lo, hi, E4X4, xcs[pi % 2], xss[pi % 2], d - c0, 256 * j))
+            last_unit.append(len(units) - 1)
         n_units = len(units)
-        first_unit = [2 + 2 * pi for pi in range(5)]
-        last_unit = [3, 5, 7, 9, 10]
 
         def load(u):
             src, cb = units[u][0], units[u][1]
@@ -88,44 +94,58 @@ def tile_scatterhorizontal_kernel(tc, x0, x1, x2, x3, x4, x5, x6, x7, x8, weight
             n = hi - lo
             raw = raws[u % 3]
             bt = bts[u % 3]
-            q = qs[u % 3]
+            qa, qb = qs[u % 3]
             a_view = raw[:, HALF:HALF + ROW].rearrange("p (k g t w) -> p g k t w", g=2, t=4, w=W)
             b_view = raw[:, 0:129 * HW].rearrange("p (k g t w) -> p g k t w", g=2, t=4, w=W)
             parts = (n + 3) // 4
             cuts = [(n * j) // parts for j in range(parts + 1)]
+            bt_flat = bt[:].rearrange("p c k t -> p (c k t)")
+            qa_flat = qa[:].rearrange("p c k t -> p (c k t)")
+            qb_flat = qb[:].rearrange("p c k t -> p (c k t)")
+
+            def exchange(e0, e1):
+                f0, f1 = e0 * PITCH * 4, e1 * PITCH * 4
+                nc.vector.tensor_copy(out=qb_flat[:, f0:f1], in_=qa_flat[:, f0:f1])
+                nc.scalar.dma_start(out=qa_flat[1:P:2, f0:f1 - 4], in_=bt_flat[0:P:2, f0 + 4:f1])
+                nc.scalar.dma_start(out=qb_flat[0:P:2, f0:f1], in_=bt_flat[1:P:2, f0:f1])
+
             for j in range(parts):
                 e0, e1 = cuts[j], cuts[j + 1]
                 nc.vector.tensor_copy(
-                    out=q[:, e0:e1, 0, :, :].rearrange("p c k t -> p k t c"),
+                    out=qa[:, e0:e1, 0:128, :].rearrange("p c k t -> p k t c"),
                     in_=a_view[:, 0, :, :, lo + e0:lo + e1],
                 )
                 nc.scalar.copy(
-                    out=bt[:, e0:e1, :, :].rearrange("p c k t -> p k t c"),
+                    out=bt[:, e0:e1, 0:129, :].rearrange("p c k t -> p k t c"),
                     in_=b_view[:, 0, :, :, lo + e0:lo + e1],
                 )
-            nc.vector.tensor_copy(out=q[:, 0:n, 1, :, :], in_=q[:, 0:n, 0, :, :])
-            nc.scalar.dma_start(out=q[1:P:2, 0:n, 0, :, :], in_=bt[0:P:2, 0:n, 1:129, :])
-            nc.scalar.dma_start(out=q[0:P:2, 0:n, 1, :, :], in_=bt[1:P:2, 0:n, 0:128, :])
+                if u == n_units - 1:
+                    exchange(e0, e1)
+            if u < n_units - 1:
+                exchange(0, n)
 
         def zero_slots(pi):
             c0, c1 = bounds[pi]
-            for j, i in enumerate(pairs[pi]):
-                d, lo, hi = span(i)
+            for j in range(2):
                 for cp in range(c0, c1):
-                    if cp < lo + d or cp >= hi + d:
+                    empty = j >= len(pairs[pi])
+                    if not empty:
+                        d, lo, hi = span(pairs[pi][j])
+                        empty = cp < lo + d or cp >= hi + d
+                    if empty:
                         nc.vector.memset(xcs[pi % 2][:, cp - c0, 256 * j:256 * j + 256].bitcast(I32), 0)
                         nc.vector.memset(xss[pi % 2][:, cp - c0, 256 * j:256 * j + 256].bitcast(I32), 0)
 
         def quantise(u):
             lo, hi, fmt, codes, scales, shift, off = units[u][2:9]
-            q = qs[u % 3]
             for ci in range(hi - lo):
                 slot = lo + ci + shift
-                nc.vector.quantize_mx(
-                    out=codes[:, slot, off:off + 256].bitcast(fmt),
-                    scales=scales[:, slot, off:off + 256],
-                    in_=q[:, ci, :, :, :].rearrange("p s k t -> p (s k t)"),
-                )
+                for s in range(2):
+                    nc.vector.quantize_mx(
+                        out=codes[:, slot, off + 128 * s:off + 128 * s + 128].bitcast(fmt),
+                        scales=scales[:, slot, off + 128 * s:off + 128 * s + 128],
+                        in_=qs[u % 3][s][:, ci, 0:128, :].rearrange("p k t -> p (k t)"),
+                    )
 
         accs = {}
 
@@ -149,11 +169,15 @@ def tile_scatterhorizontal_kernel(tc, x0, x1, x2, x3, x4, x5, x6, x7, x8, weight
         def evac(pi):
             width = 256 * len(pairs[pi])
             for ot in range(4):
-                nc.scalar.copy(out=osts[pi][:, ot, 0:width], in_=accs[(pi, ot)][:, 0:width])
+                if pi == len(pairs) - 1 and ot % 2 == 1:
+                    nc.vector.tensor_copy(out=osts[pi][:, ot, 0:width], in_=accs[(pi, ot)][:, 0:width])
+                else:
+                    nc.scalar.copy(out=osts[pi][:, ot, 0:width], in_=accs[(pi, ot)][:, 0:width])
 
         def store(pi):
             for j, i in enumerate(pairs[pi]):
-                nc.sync.dma_start(
+                queue = nc.sync if (pi == 0 or (pi == len(pairs) - 1 and j == 1)) else nc.scalar
+                queue.dma_start(
                     out=out[i].rearrange("(t o) k -> o t k", o=P),
                     in_=osts[pi][:, :, 256 * j:256 * j + 256],
                 )
@@ -177,7 +201,7 @@ def tile_scatterhorizontal_kernel(tc, x0, x1, x2, x3, x4, x5, x6, x7, x8, weight
             if t - 4 in last_unit:
                 evac(last_unit.index(t - 4))
                 waiting.append(last_unit.index(t - 4))
-            if t + 2 >= n_units - 1:
+            if t >= n_units - 1 or 0 in waiting:
                 for pi in waiting:
                     store(pi)
                 waiting = []

@@ -115,10 +115,16 @@ def tile_scatterhorizontal_kernel(tc, x0, x1, x2, x3, x4, x5, x6, x7, x8, weight
                     out=qa[:, e0:e1, 0:128, :].rearrange("p c k t -> p k t c"),
                     in_=a_view[:, 0, :, :, lo + e0:lo + e1],
                 )
-                nc.scalar.copy(
-                    out=bt[:, e0:e1, 0:129, :].rearrange("p c k t -> p k t c"),
-                    in_=b_view[:, 0, :, :, lo + e0:lo + e1],
-                )
+                if j == 0:
+                    nc.vector.tensor_copy(
+                        out=bt[:, e0:e1, 0:129, :].rearrange("p c k t -> p k t c"),
+                        in_=b_view[:, 0, :, :, lo + e0:lo + e1],
+                    )
+                else:
+                    nc.scalar.copy(
+                        out=bt[:, e0:e1, 0:129, :].rearrange("p c k t -> p k t c"),
+                        in_=b_view[:, 0, :, :, lo + e0:lo + e1],
+                    )
                 if u == n_units - 1:
                     exchange(e0, e1)
             if u < n_units - 1:

@@ -1,12 +1,12 @@
 from contextlib import ExitStack
 
 import concourse.mybir as mybir
+from concourse.masks import make_identity
 
 BF16 = mybir.dt.bfloat16
 F32 = mybir.dt.float32
 U32 = mybir.dt.uint32
 U8 = mybir.dt.uint8
-I32 = mybir.dt.int32
 E4X4 = mybir.dt.float8_e4m3fn_x4
 E5X4 = mybir.dt.float8_e5m2_x4
 
@@ -16,7 +16,8 @@ PADW = 4
 HW = 72
 HALF = 36
 ROW = 128 * HW
-PITCH = 136
+BASE = 12
+COL = 512
 FLOPS = 2 * 61 * 512 * 512 * 256
 
 
@@ -28,168 +29,165 @@ def span(i):
 def tile_scatterhorizontal_kernel(tc, x0, x1, x2, x3, x4, x5, x6, x7, x8, weights, bias, grad_out, out):
     nc = tc.nc
     xs = [x0, x1, x2, x3, x4, x5, x6, x7, x8]
-    pairs = [(0,), (1, 2), (3, 4), (5, 6), (7, 8)]
     with ExitStack() as ctx:
         keep = ctx.enter_context(tc.tile_pool(name="keep", bufs=1))
-        psum = ctx.enter_context(tc.psum_pool(name="psum", bufs=8))
+        mid = ctx.enter_context(tc.tile_pool(name="mid", bufs=2))
+        psum_a = ctx.enter_context(tc.psum_pool(name="psum_a", bufs=4))
+        psum_t = ctx.enter_context(tc.psum_pool(name="psum_t", bufs=4))
         ctx.enter_context(tc.manual_schedule())
 
+        ident = keep.tile([P, P], F32, name="ident")
+        make_identity(nc, ident[:])
         raws = []
         bts = []
         qs = []
-        for j in range(3):
-            cols = W if j < 2 else W - 1
-            raw_t = keep.tile([P, 129 * HW], BF16, name="raw%d" % j)
-            bt_t = keep.tile([P, cols, PITCH, 4], BF16, name="bt%d" % j)
-            qa_t = keep.tile([P, cols, PITCH, 4], BF16, name="qa%d" % j, align_bytes=64)
-            qb_t = keep.tile([P, cols, PITCH, 4], BF16, name="qb%d" % j, align_bytes=64)
-            nc.vector.memset(raw_t[:, 0:48], 0.0)
-            nc.vector.memset(raw_t[:, ROW:ROW + HW], 0.0)
-            nc.vector.memset(bt_t[:, :, 128:PITCH, :], 0.0)
-            nc.vector.memset(qa_t[:, :, 128:PITCH, :], 0.0)
-            raws.append(raw_t)
-            bts.append(bt_t)
-            qs.append((qa_t, qb_t))
         xcs = []
         xss = []
-        for j in range(2):
-            xc_t = keep.tile([P, W - j, 512], U32, name="xc%d" % j, align_bytes=64)
-            xs_t = keep.tile([P, W - j, 512], U8, name="xs%d" % j, align_bytes=64)
+        for j in range(3):
+            cols = W if j < 2 else W - 1
+            raw_t = keep.tile([P, BASE + HALF + ROW], BF16, name="raw%d" % j)
+            bt_t = keep.tile([P, cols * COL + 16], BF16, name="bt%d" % j)
+            q_t = keep.tile([P, 2 * cols * COL], BF16, name="q%d" % j, align_bytes=64)
+            xc_t = keep.tile([P, 2 * cols * P], U32, name="xc%d" % j, align_bytes=64)
+            xs_t = keep.tile([P, 2 * cols * P], U8, name="xs%d" % j, align_bytes=64)
+            nc.vector.memset(raw_t[:, 0:16], 0.0)
+            nc.vector.memset(raw_t[:, BASE + ROW - 12:BASE + ROW + HALF], 0.0)
+            raws.append(raw_t)
+            bts.append(bt_t)
+            qs.append(q_t)
             xcs.append(xc_t)
             xss.append(xs_t)
         gc = keep.tile([P, W, 512], U32, name="gc", align_bytes=64)
         gs = keep.tile([P, W, 512], U8, name="gs", align_bytes=64)
         osts = []
-        for j in range(4):
-            ost_t = keep.tile([P, 4, 512], F32, name="ost%d" % j)
+        for j in range(7):
+            ost_t = keep.tile([P, 4, 256], F32, name="ost%d" % j)
             osts.append(ost_t)
-        osts = [osts[3]] + osts
 
-        units = []
-        for half in range(2):
-            units.append((grad_out, 256 * half, 0, W, E5X4, gc, gs, 0, 256 * half))
-        bounds = []
-        first_unit = []
-        last_unit = []
-        for pi, pair in enumerate(pairs):
-            c0 = min(span(i)[1] + span(i)[0] for i in pair)
-            c1 = max(span(i)[2] + span(i)[0] for i in pair)
-            bounds.append((c0, c1))
-            first_unit.append(len(units))
-            for j, i in enumerate(pair):
-                d, lo, hi = span(i)
-                units.append((xs[i], 0, lo, hi, E4X4, xcs[pi % 2], xss[pi % 2], d - c0, 256 * j))
-            last_unit.append(len(units) - 1)
+        units = [(grad_out, 0, 0, W), (grad_out, 256, 0, W)]
+        for i in range(9):
+            d, lo, hi = span(i)
+            units.append((xs[i], 0, lo, hi))
         n_units = len(units)
 
         def load(u):
             src, cb = units[u][0], units[u][1]
             raw = raws[u % 3]
             flat = src.rearrange("b k h w -> b (k h w)")
-            nc.sync.dma_start(out=raw[0:P:2, HALF:HALF + ROW], in_=flat[:, cb * HW:cb * HW + ROW])
-            nc.sync.dma_start(out=raw[1:P:2, 0:ROW], in_=flat[:, (cb + 128) * HW:(cb + 128) * HW + ROW])
+            e0 = cb * HW
+            o0 = (cb + 128) * HW
+            nc.sync.dma_start(out=raw[0:P:2, BASE + HALF:BASE + HALF + ROW], in_=flat[:, e0:e0 + ROW])
+            nc.sync.dma_start(out=raw[1:P:2, BASE:BASE + ROW], in_=flat[:, o0:o0 + ROW])
+            nc.sync.dma_start(out=raw[0:P:2, BASE + 1:BASE + HALF], in_=flat[:, e0 + ROW - HALF:e0 + ROW - 1])
 
         def regroup(u):
             lo, hi = units[u][2], units[u][3]
             n = hi - lo
             raw = raws[u % 3]
             bt = bts[u % 3]
-            qa, qb = qs[u % 3]
-            a_view = raw[:, HALF:HALF + ROW].rearrange("p (k g t w) -> p g k t w", g=2, t=4, w=W)
-            b_view = raw[:, 0:129 * HW].rearrange("p (k g t w) -> p g k t w", g=2, t=4, w=W)
+            q = qs[u % 3]
+            a_view = raw[:, BASE + HALF:BASE + HALF + ROW].rearrange("p (k g t w) -> p g k t w", g=2, t=4, w=W)
+            b_view = raw[:, BASE:BASE + ROW].rearrange("p (k g t w) -> p g k t w", g=2, t=4, w=W)
+            tail = raw[:, BASE + ROW:BASE + ROW + HALF].rearrange("p (t w) -> p t w", w=W)
             parts = (n + 3) // 4
             cuts = [(n * j) // parts for j in range(parts + 1)]
-            bt_flat = bt[:].rearrange("p c k t -> p (c k t)")
-            qa_flat = qa[:].rearrange("p c k t -> p (c k t)")
-            qb_flat = qb[:].rearrange("p c k t -> p (c k t)")
-
-            def exchange(e0, e1):
-                f0, f1 = e0 * PITCH * 4, e1 * PITCH * 4
-                nc.vector.tensor_copy(out=qb_flat[:, f0:f1], in_=qa_flat[:, f0:f1])
-                nc.scalar.dma_start(out=qa_flat[1:P:2, f0:f1 - 4], in_=bt_flat[0:P:2, f0 + 4:f1])
-                nc.scalar.dma_start(out=qb_flat[0:P:2, f0:f1], in_=bt_flat[1:P:2, f0:f1])
-
             for j in range(parts):
                 e0, e1 = cuts[j], cuts[j + 1]
                 nc.vector.tensor_copy(
-                    out=qa[:, e0:e1, 0:128, :].rearrange("p c k t -> p k t c"),
+                    out=q[:, e0 * COL:e1 * COL].rearrange("p (c k t) -> p k t c", k=128, t=4),
                     in_=a_view[:, 0, :, :, lo + e0:lo + e1],
                 )
-                if j == 0:
-                    nc.vector.tensor_copy(
-                        out=bt[:, e0:e1, 0:129, :].rearrange("p c k t -> p k t c"),
-                        in_=b_view[:, 0, :, :, lo + e0:lo + e1],
-                    )
-                else:
-                    nc.scalar.copy(
-                        out=bt[:, e0:e1, 0:129, :].rearrange("p c k t -> p k t c"),
-                        in_=b_view[:, 0, :, :, lo + e0:lo + e1],
-                    )
-                if u == n_units - 1:
-                    exchange(e0, e1)
-            if u < n_units - 1:
-                exchange(0, n)
-
-        def zero_slots(pi):
-            c0, c1 = bounds[pi]
-            for j in range(2):
-                for cp in range(c0, c1):
-                    empty = j >= len(pairs[pi])
-                    if not empty:
-                        d, lo, hi = span(pairs[pi][j])
-                        empty = cp < lo + d or cp >= hi + d
-                    if empty:
-                        nc.vector.memset(xcs[pi % 2][:, cp - c0, 256 * j:256 * j + 256].bitcast(I32), 0)
-                        nc.vector.memset(xss[pi % 2][:, cp - c0, 256 * j:256 * j + 256].bitcast(I32), 0)
+                nc.scalar.copy(
+                    out=bt[:, e0 * COL:e1 * COL].rearrange("p (c k t) -> p k t c", k=128, t=4),
+                    in_=b_view[:, 0, :, :, lo + e0:lo + e1],
+                )
+            nc.scalar.copy(out=bt[:, n * COL:n * COL + 4], in_=tail[:, :, hi - 1])
+            nc.vector.tensor_copy(out=q[:, n * COL:2 * n * COL], in_=q[:, 0:n * COL])
+            nc.scalar.dma_start(out=q[1:P:2, 0:n * COL], in_=bt[0:P:2, 4:n * COL + 4])
+            nc.scalar.dma_start(out=q[0:P:2, n * COL:2 * n * COL], in_=bt[1:P:2, 0:n * COL])
 
         def quantise(u):
-            lo, hi, fmt, codes, scales, shift, off = units[u][2:9]
-            for ci in range(hi - lo):
-                slot = lo + ci + shift
+            n = units[u][3] - units[u][2]
+            q = qs[u % 3]
+            if u < 2:
                 for s in range(2):
-                    nc.vector.quantize_mx(
-                        out=codes[:, slot, off + 128 * s:off + 128 * s + 128].bitcast(fmt),
-                        scales=scales[:, slot, off + 128 * s:off + 128 * s + 128],
-                        in_=qs[u % 3][s][:, ci, 0:128, :].rearrange("p k t -> p (k t)"),
-                    )
+                    for c in range(n):
+                        f = (s * n + c) * COL
+                        w0 = 256 * u + 128 * s
+                        nc.vector.quantize_mx(
+                            out=gc[:, c, w0:w0 + 128].bitcast(E5X4),
+                            scales=gs[:, c, w0:w0 + 128],
+                            in_=q[:, f:f + COL],
+                        )
+                return
+            f = 0
+            while f < 2 * n * COL:
+                width = 4096
+                while f + width > 2 * n * COL:
+                    width = width // 2
+                nc.vector.quantize_mx(
+                    out=xcs[u % 3][:, f // 4:(f + width) // 4].bitcast(E4X4),
+                    scales=xss[u % 3][:, f // 4:(f + width) // 4],
+                    in_=q[:, f:f + width],
+                )
+                f += width
 
         accs = {}
+        t1s = {}
+        pts = {}
 
-        def matmuls(pi):
-            c0, c1 = bounds[pi]
-            for ot in range(4):
-                acc = psum.tile([P, 512], F32, tag="acc")
-                accs[(pi, ot)] = acc
-            for cp in range(c0, c1):
-                for ot in range(4):
+        def matmuls(u):
+            lo, hi = units[u][2], units[u][3]
+            n = hi - lo
+            d = u - 2 - PADW
+            for s in range(2):
+                acc = psum_a.tile([P, 512], F32, tag="acc")
+                accs[(u, s)] = acc
+                for c in range(n):
+                    w0 = (s * n + c) * P
                     nc.tensor.matmul_mx(
-                        out=accs[(pi, ot)][:],
-                        lhsT=gc[:, cp, 128 * ot:128 * ot + 128].bitcast(E5X4),
-                        lhsT_scale=gs[:, cp, 128 * ot:128 * ot + 128],
-                        rhs=xcs[pi % 2][:, cp - c0, :].bitcast(E4X4),
-                        rhs_scale=xss[pi % 2][:, cp - c0, :],
-                        start=(cp == c0),
-                        stop=(cp == c1 - 1),
+                        out=acc[:],
+                        lhsT=xcs[u % 3][:, w0:w0 + P].bitcast(E4X4),
+                        lhsT_scale=xss[u % 3][:, w0:w0 + P],
+                        rhs=gc[:, lo + c + d, :].bitcast(E5X4),
+                        rhs_scale=gs[:, lo + c + d, :],
+                        start=(c == 0),
+                        stop=(c == n - 1),
                     )
 
-        def evac(pi):
-            width = 256 * len(pairs[pi])
-            for ot in range(4):
-                if pi == len(pairs) - 1 and ot % 2 == 1:
-                    nc.vector.tensor_copy(out=osts[pi][:, ot, 0:width], in_=accs[(pi, ot)][:, 0:width])
-                else:
-                    nc.scalar.copy(out=osts[pi][:, ot, 0:width], in_=accs[(pi, ot)][:, 0:width])
+        def evac1(u):
+            t1 = mid.tile([P, 2, 512], F32, tag="t1")
+            t1s[u] = t1
+            nc.scalar.copy(out=t1[:, 0, :], in_=accs[(u, 0)][:])
+            if u == n_units - 1:
+                nc.vector.tensor_copy(out=t1[:, 1, :], in_=accs[(u, 1)][:])
+            else:
+                nc.scalar.copy(out=t1[:, 1, :], in_=accs[(u, 1)][:])
 
-        def store(pi):
-            for j, i in enumerate(pairs[pi]):
-                queue = nc.sync if (pi == 0 or (pi == len(pairs) - 1 and j == 1)) else nc.scalar
-                queue.dma_start(
-                    out=out[i].rearrange("(t o) k -> o t k", o=P),
-                    in_=osts[pi][:, :, 256 * j:256 * j + 256],
-                )
+        def transposes(u):
+            for h in range(2):
+                pt = psum_t.tile([P, 2, 2, P], F32, tag="pt")
+                pts[(u, h)] = pt
+                for o2 in range(2):
+                    for s in range(2):
+                        ot = 2 * h + o2
+                        nc.tensor.transpose(pt[:, o2, s, :], t1s[u][:, s, P * ot:P * ot + P], ident[:])
 
+        def evac2(u):
+            ost = osts[(u - 2) % 7]
+            nc.scalar.copy(out=ost[:, 0:2, :], in_=pts[(u, 0)][:].rearrange("p a s k -> p a (s k)"))
+            if u == n_units - 1:
+                nc.vector.tensor_copy(out=ost[:, 2:4, :], in_=pts[(u, 1)][:].rearrange("p a s k -> p a (s k)"))
+            else:
+                nc.scalar.copy(out=ost[:, 2:4, :], in_=pts[(u, 1)][:].rearrange("p a s k -> p a (s k)"))
+
+        def store(u):
+            queue = nc.sync if u < 4 else nc.scalar
+            queue.dma_start(out=out[u - 2].rearrange("(t o) k -> o t k", o=P), in_=osts[(u - 2) % 7][:])
+
+        z_next = 0
         waiting = []
-        for t in range(n_units + 5):
+        for t in range(n_units + 6):
             if t == 0:
                 load(0)
                 load(1)
@@ -197,17 +195,21 @@ def tile_scatterhorizontal_kernel(tc, x0, x1, x2, x3, x4, x5, x6, x7, x8, weight
                 load(t + 2)
             if t < n_units:
                 regroup(t)
-            z = t - 2
-            if 0 <= z < n_units:
-                if z in first_unit:
-                    zero_slots(first_unit.index(z))
-                quantise(z)
-                if z in last_unit:
-                    matmuls(last_unit.index(z))
-            if t - 4 in last_unit:
-                evac(last_unit.index(t - 4))
-                waiting.append(last_unit.index(t - 4))
-            if t >= n_units - 1 or 0 in waiting:
-                for pi in waiting:
-                    store(pi)
+            z_end = t - 1 if t >= 9 else t - 2
+            while z_next <= min(z_end, n_units - 1):
+                quantise(z_next)
+                if z_next >= 2:
+                    matmuls(z_next)
+                z_next += 1
+            e_unit = t - 3
+            if 2 <= e_unit < n_units:
+                evac1(e_unit)
+                transposes(e_unit)
+            f_unit = t - 4
+            if 2 <= f_unit < n_units:
+                evac2(f_unit)
+                waiting.append(f_unit)
+            if t >= n_units - 1 or (waiting and waiting[0] < 4):
+                for u in waiting:
+                    store(u)
                 waiting = []

@@ -18,6 +18,7 @@ HALF = 36
 ROW = 128 * HW
 BASE = 12
 COL = 512
+LAST_CUTS = [0, 3, 5]
 FLOPS = 2 * 61 * 512 * 512 * 256
 
 
@@ -31,7 +32,7 @@ def tile_scatterhorizontal_kernel(tc, x0, x1, x2, x3, x4, x5, x6, x7, x8, weight
     xs = [x0, x1, x2, x3, x4, x5, x6, x7, x8]
     with ExitStack() as ctx:
         keep = ctx.enter_context(tc.tile_pool(name="keep", bufs=1))
-        mid = ctx.enter_context(tc.tile_pool(name="mid", bufs=2))
+        mid = ctx.enter_context(tc.tile_pool(name="mid", bufs=3))
         psum_a = ctx.enter_context(tc.psum_pool(name="psum_a", bufs=4))
         psum_t = ctx.enter_context(tc.psum_pool(name="psum_t", bufs=4))
         ctx.enter_context(tc.manual_schedule())
@@ -46,7 +47,7 @@ def tile_scatterhorizontal_kernel(tc, x0, x1, x2, x3, x4, x5, x6, x7, x8, weight
         for j in range(3):
             cols = W if j < 2 else W - 1
             raw_t = keep.tile([P, BASE + HALF + ROW], BF16, name="raw%d" % j)
-            bt_t = keep.tile([P, cols * COL + 16], BF16, name="bt%d" % j)
+            bt_t = keep.tile([P, cols * COL + 32], BF16, name="bt%d" % j)
             q_t = keep.tile([P, 2 * cols * COL], BF16, name="q%d" % j, align_bytes=64)
             xc_t = keep.tile([P, 2 * cols * P], U32, name="xc%d" % j, align_bytes=64)
             xs_t = keep.tile([P, 2 * cols * P], U8, name="xs%d" % j, align_bytes=64)
@@ -65,7 +66,8 @@ def tile_scatterhorizontal_kernel(tc, x0, x1, x2, x3, x4, x5, x6, x7, x8, weight
             osts.append(ost_t)
 
         units = [(grad_out, 0, 0, W), (grad_out, 256, 0, W)]
-        for i in range(9):
+        order = [3, 4, 5, 2, 6, 1, 7, 0, 8]
+        for i in order:
             d, lo, hi = span(i)
             units.append((xs[i], 0, lo, hi))
         n_units = len(units)
@@ -91,20 +93,32 @@ def tile_scatterhorizontal_kernel(tc, x0, x1, x2, x3, x4, x5, x6, x7, x8, weight
             tail = raw[:, BASE + ROW:BASE + ROW + HALF].rearrange("p (t w) -> p t w", w=W)
             parts = (n + 3) // 4
             cuts = [(n * j) // parts for j in range(parts + 1)]
-            for j in range(parts):
+            split = u == n_units - 1
+            if split:
+                cuts = LAST_CUTS
+
+            def exchange(e0, e1, b0):
+                size = (e1 - e0) * COL
+                nc.scalar.copy(out=bt[:, b0 + size:b0 + size + 4], in_=tail[:, :, lo + e1 - 1])
+                nc.vector.tensor_copy(out=q[:, (n + e0) * COL:(n + e1) * COL], in_=q[:, e0 * COL:e1 * COL])
+                nc.scalar.dma_start(out=q[1:P:2, e0 * COL:e1 * COL], in_=bt[0:P:2, b0 + 4:b0 + size + 4])
+                nc.scalar.dma_start(out=q[0:P:2, (n + e0) * COL:(n + e1) * COL], in_=bt[1:P:2, b0:b0 + size])
+
+            for j in range(len(cuts) - 1):
                 e0, e1 = cuts[j], cuts[j + 1]
+                b0 = e0 * COL + (16 * j if split else 0)
                 nc.vector.tensor_copy(
                     out=q[:, e0 * COL:e1 * COL].rearrange("p (c k t) -> p k t c", k=128, t=4),
                     in_=a_view[:, 0, :, :, lo + e0:lo + e1],
                 )
                 nc.scalar.copy(
-                    out=bt[:, e0 * COL:e1 * COL].rearrange("p (c k t) -> p k t c", k=128, t=4),
+                    out=bt[:, b0:b0 + (e1 - e0) * COL].rearrange("p (c k t) -> p k t c", k=128, t=4),
                     in_=b_view[:, 0, :, :, lo + e0:lo + e1],
                 )
-            nc.scalar.copy(out=bt[:, n * COL:n * COL + 4], in_=tail[:, :, hi - 1])
-            nc.vector.tensor_copy(out=q[:, n * COL:2 * n * COL], in_=q[:, 0:n * COL])
-            nc.scalar.dma_start(out=q[1:P:2, 0:n * COL], in_=bt[0:P:2, 4:n * COL + 4])
-            nc.scalar.dma_start(out=q[0:P:2, n * COL:2 * n * COL], in_=bt[1:P:2, 0:n * COL])
+                if split:
+                    exchange(e0, e1, b0)
+            if not split:
+                exchange(0, n, 0)
 
         def quantise(u):
             n = units[u][3] - units[u][2]
@@ -120,10 +134,13 @@ def tile_scatterhorizontal_kernel(tc, x0, x1, x2, x3, x4, x5, x6, x7, x8, weight
                             in_=q[:, f:f + COL],
                         )
                 return
-            f = 0
-            while f < 2 * n * COL:
+            quantise_range(u, 0, 2 * n * COL)
+
+        def quantise_range(u, f, end):
+            q = qs[u % 3]
+            while f < end:
                 width = 4096
-                while f + width > 2 * n * COL:
+                while f + width > end:
                     width = width // 2
                 nc.vector.quantize_mx(
                     out=xcs[u % 3][:, f // 4:(f + width) // 4].bitcast(E4X4),
@@ -139,14 +156,21 @@ def tile_scatterhorizontal_kernel(tc, x0, x1, x2, x3, x4, x5, x6, x7, x8, weight
         def matmuls(u):
             lo, hi = units[u][2], units[u][3]
             n = hi - lo
-            d = u - 2 - PADW
+            d = order[u - 2] - PADW
             for s in range(2):
                 acc = psum_a.tile([P, 512], F32, tag="acc")
                 accs[(u, s)] = acc
-                for c in range(n):
+                passes(u, s, 0, n)
+
+        def passes(u, s, e0, e1):
+            lo, hi = units[u][2], units[u][3]
+            n = hi - lo
+            d = order[u - 2] - PADW
+            if True:
+                for c in range(e0, e1):
                     w0 = (s * n + c) * P
                     nc.tensor.matmul_mx(
-                        out=acc[:],
+                        out=accs[(u, s)][:],
                         lhsT=xcs[u % 3][:, w0:w0 + P].bitcast(E4X4),
                         lhsT_scale=xss[u % 3][:, w0:w0 + P],
                         rhs=gc[:, lo + c + d, :].bitcast(E5X4),
@@ -176,18 +200,25 @@ def tile_scatterhorizontal_kernel(tc, x0, x1, x2, x3, x4, x5, x6, x7, x8, weight
         def evac2(u):
             ost = osts[(u - 2) % 7]
             nc.scalar.copy(out=ost[:, 0:2, :], in_=pts[(u, 0)][:].rearrange("p a s k -> p a (s k)"))
-            if u == n_units - 1:
+            if u >= n_units - 3:
                 nc.vector.tensor_copy(out=ost[:, 2:4, :], in_=pts[(u, 1)][:].rearrange("p a s k -> p a (s k)"))
             else:
                 nc.scalar.copy(out=ost[:, 2:4, :], in_=pts[(u, 1)][:].rearrange("p a s k -> p a (s k)"))
 
         def store(u):
-            queue = nc.sync if u < 4 else nc.scalar
-            queue.dma_start(out=out[u - 2].rearrange("(t o) k -> o t k", o=P), in_=osts[(u - 2) % 7][:])
+            dst = out[order[u - 2]].rearrange("(t o) k -> o t k", o=P)
+            ost = osts[(u - 2) % 7]
+            if u == n_units - 1:
+                nc.scalar.dma_start(out=dst[:, 0:2, :], in_=ost[:, 0:2, :])
+                nc.sync.dma_start(out=dst[:, 2:4, :], in_=ost[:, 2:4, :])
+            elif u <= 4:
+                nc.sync.dma_start(out=dst, in_=ost[:])
+            else:
+                nc.scalar.dma_start(out=dst, in_=ost[:])
 
         z_next = 0
         waiting = []
-        for t in range(n_units + 6):
+        for t in range(n_units - 1):
             if t == 0:
                 load(0)
                 load(1)
@@ -209,7 +240,40 @@ def tile_scatterhorizontal_kernel(tc, x0, x1, x2, x3, x4, x5, x6, x7, x8, weight
             if 2 <= f_unit < n_units:
                 evac2(f_unit)
                 waiting.append(f_unit)
-            if t >= n_units - 1 or (waiting and waiting[0] < 4):
+            if t == n_units - 3:
                 for u in waiting:
                     store(u)
                 waiting = []
+
+        last = n_units - 1
+        n_last = units[last][3] - units[last][2]
+        regroup(last)
+        quantise(last - 1)
+        matmuls(last - 1)
+        evac1(last - 3)
+        transposes(last - 3)
+        evac2(last - 4)
+        for u in waiting + [last - 4]:
+            store(u)
+        evac1(last - 2)
+        for s in range(2):
+            acc = psum_a.tile([P, 512], F32, tag="acc")
+            accs[(last, s)] = acc
+        for j in range(len(LAST_CUTS) - 1):
+            e0, e1 = LAST_CUTS[j], LAST_CUTS[j + 1]
+            for s in range(2):
+                quantise_range(last, (s * n_last + e0) * COL, (s * n_last + e1) * COL)
+                passes(last, s, e0, e1)
+        evac1(last - 1)
+        evac2(last - 3)
+        store(last - 3)
+        transposes(last - 2)
+        transposes(last - 1)
+        evac1(last)
+        evac2(last - 2)
+        store(last - 2)
+        evac2(last - 1)
+        store(last - 1)
+        transposes(last)
+        evac2(last)
+        store(last)

@@ -18,7 +18,6 @@ HALF = 36
 ROW = 128 * HW
 BASE = 12
 COL = 512
-LAST_CUTS = [0, 3, 5]
 FLOPS = 2 * 61 * 512 * 512 * 256
 
 
@@ -32,7 +31,7 @@ def tile_scatterhorizontal_kernel(tc, x0, x1, x2, x3, x4, x5, x6, x7, x8, weight
     xs = [x0, x1, x2, x3, x4, x5, x6, x7, x8]
     with ExitStack() as ctx:
         keep = ctx.enter_context(tc.tile_pool(name="keep", bufs=1))
-        mid = ctx.enter_context(tc.tile_pool(name="mid", bufs=3))
+        mid = ctx.enter_context(tc.tile_pool(name="mid", bufs=2))
         psum_a = ctx.enter_context(tc.psum_pool(name="psum_a", bufs=4))
         psum_t = ctx.enter_context(tc.psum_pool(name="psum_t", bufs=4))
         ctx.enter_context(tc.manual_schedule())
@@ -47,7 +46,7 @@ def tile_scatterhorizontal_kernel(tc, x0, x1, x2, x3, x4, x5, x6, x7, x8, weight
         for j in range(3):
             cols = W if j < 2 else W - 1
             raw_t = keep.tile([P, BASE + HALF + ROW], BF16, name="raw%d" % j)
-            bt_t = keep.tile([P, cols * COL + 32], BF16, name="bt%d" % j)
+            bt_t = keep.tile([P, cols * COL + 16], BF16, name="bt%d" % j)
             q_t = keep.tile([P, 2 * cols * COL], BF16, name="q%d" % j, align_bytes=64)
             xc_t = keep.tile([P, 2 * cols * P], U32, name="xc%d" % j, align_bytes=64)
             xs_t = keep.tile([P, 2 * cols * P], U8, name="xs%d" % j, align_bytes=64)
@@ -93,32 +92,20 @@ def tile_scatterhorizontal_kernel(tc, x0, x1, x2, x3, x4, x5, x6, x7, x8, weight
             tail = raw[:, BASE + ROW:BASE + ROW + HALF].rearrange("p (t w) -> p t w", w=W)
             parts = (n + 3) // 4
             cuts = [(n * j) // parts for j in range(parts + 1)]
-            split = u == n_units - 1
-            if split:
-                cuts = LAST_CUTS
-
-            def exchange(e0, e1, b0):
-                size = (e1 - e0) * COL
-                nc.scalar.copy(out=bt[:, b0 + size:b0 + size + 4], in_=tail[:, :, lo + e1 - 1])
-                nc.vector.tensor_copy(out=q[:, (n + e0) * COL:(n + e1) * COL], in_=q[:, e0 * COL:e1 * COL])
-                nc.scalar.dma_start(out=q[1:P:2, e0 * COL:e1 * COL], in_=bt[0:P:2, b0 + 4:b0 + size + 4])
-                nc.scalar.dma_start(out=q[0:P:2, (n + e0) * COL:(n + e1) * COL], in_=bt[1:P:2, b0:b0 + size])
-
-            for j in range(len(cuts) - 1):
+            for j in range(parts):
                 e0, e1 = cuts[j], cuts[j + 1]
-                b0 = e0 * COL + (16 * j if split else 0)
                 nc.vector.tensor_copy(
                     out=q[:, e0 * COL:e1 * COL].rearrange("p (c k t) -> p k t c", k=128, t=4),
                     in_=a_view[:, 0, :, :, lo + e0:lo + e1],
                 )
                 nc.scalar.copy(
-                    out=bt[:, b0:b0 + (e1 - e0) * COL].rearrange("p (c k t) -> p k t c", k=128, t=4),
+                    out=bt[:, e0 * COL:e1 * COL].rearrange("p (c k t) -> p k t c", k=128, t=4),
                     in_=b_view[:, 0, :, :, lo + e0:lo + e1],
                 )
-                if split:
-                    exchange(e0, e1, b0)
-            if not split:
-                exchange(0, n, 0)
+            nc.scalar.copy(out=bt[:, n * COL:n * COL + 4], in_=tail[:, :, hi - 1])
+            nc.vector.tensor_copy(out=q[:, n * COL:2 * n * COL], in_=q[:, 0:n * COL])
+            nc.scalar.dma_start(out=q[1:P:2, 0:n * COL], in_=bt[0:P:2, 4:n * COL + 4])
+            nc.scalar.dma_start(out=q[0:P:2, n * COL:2 * n * COL], in_=bt[1:P:2, 0:n * COL])
 
         def quantise(u):
             n = units[u][3] - units[u][2]
@@ -134,13 +121,10 @@ def tile_scatterhorizontal_kernel(tc, x0, x1, x2, x3, x4, x5, x6, x7, x8, weight
                             in_=q[:, f:f + COL],
                         )
                 return
-            quantise_range(u, 0, 2 * n * COL)
-
-        def quantise_range(u, f, end):
-            q = qs[u % 3]
-            while f < end:
+            f = 0
+            while f < 2 * n * COL:
                 width = 4096
-                while f + width > end:
+                while f + width > 2 * n * COL:
                     width = width // 2
                 nc.vector.quantize_mx(
                     out=xcs[u % 3][:, f // 4:(f + width) // 4].bitcast(E4X4),
@@ -160,17 +144,10 @@ def tile_scatterhorizontal_kernel(tc, x0, x1, x2, x3, x4, x5, x6, x7, x8, weight
             for s in range(2):
                 acc = psum_a.tile([P, 512], F32, tag="acc")
                 accs[(u, s)] = acc
-                passes(u, s, 0, n)
-
-        def passes(u, s, e0, e1):
-            lo, hi = units[u][2], units[u][3]
-            n = hi - lo
-            d = order[u - 2] - PADW
-            if True:
-                for c in range(e0, e1):
+                for c in range(n):
                     w0 = (s * n + c) * P
                     nc.tensor.matmul_mx(
-                        out=accs[(u, s)][:],
+                        out=acc[:],
                         lhsT=xcs[u % 3][:, w0:w0 + P].bitcast(E4X4),
                         lhsT_scale=xss[u % 3][:, w0:w0 + P],
                         rhs=gc[:, lo + c + d, :].bitcast(E5X4),
@@ -200,7 +177,7 @@ def tile_scatterhorizontal_kernel(tc, x0, x1, x2, x3, x4, x5, x6, x7, x8, weight
         def evac2(u):
             ost = osts[(u - 2) % 7]
             nc.scalar.copy(out=ost[:, 0:2, :], in_=pts[(u, 0)][:].rearrange("p a s k -> p a (s k)"))
-            if u >= n_units - 3:
+            if u == n_units - 1:
                 nc.vector.tensor_copy(out=ost[:, 2:4, :], in_=pts[(u, 1)][:].rearrange("p a s k -> p a (s k)"))
             else:
                 nc.scalar.copy(out=ost[:, 2:4, :], in_=pts[(u, 1)][:].rearrange("p a s k -> p a (s k)"))
@@ -218,7 +195,7 @@ def tile_scatterhorizontal_kernel(tc, x0, x1, x2, x3, x4, x5, x6, x7, x8, weight
 
         z_next = 0
         waiting = []
-        for t in range(n_units - 1):
+        for t in range(n_units + 6):
             if t == 0:
                 load(0)
                 load(1)
@@ -240,40 +217,7 @@ def tile_scatterhorizontal_kernel(tc, x0, x1, x2, x3, x4, x5, x6, x7, x8, weight
             if 2 <= f_unit < n_units:
                 evac2(f_unit)
                 waiting.append(f_unit)
-            if t == n_units - 3:
+            if t >= n_units - 1 or t == n_units - 3:
                 for u in waiting:
                     store(u)
                 waiting = []
-
-        last = n_units - 1
-        n_last = units[last][3] - units[last][2]
-        regroup(last)
-        quantise(last - 1)
-        matmuls(last - 1)
-        evac1(last - 3)
-        transposes(last - 3)
-        evac2(last - 4)
-        for u in waiting + [last - 4]:
-            store(u)
-        evac1(last - 2)
-        for s in range(2):
-            acc = psum_a.tile([P, 512], F32, tag="acc")
-            accs[(last, s)] = acc
-        for j in range(len(LAST_CUTS) - 1):
-            e0, e1 = LAST_CUTS[j], LAST_CUTS[j + 1]
-            for s in range(2):
-                quantise_range(last, (s * n_last + e0) * COL, (s * n_last + e1) * COL)
-                passes(last, s, e0, e1)
-        evac1(last - 1)
-        evac2(last - 3)
-        store(last - 3)
-        transposes(last - 2)
-        transposes(last - 1)
-        evac1(last)
-        evac2(last - 2)
-        store(last - 2)
-        evac2(last - 1)
-        store(last - 1)
-        transposes(last)
-        evac2(last)
-        store(last)

@@ -7,217 +7,213 @@ BF16 = mybir.dt.bfloat16
 F32 = mybir.dt.float32
 U32 = mybir.dt.uint32
 U8 = mybir.dt.uint8
-E4X4 = mybir.dt.float8_e4m3fn_x4
-E5X4 = mybir.dt.float8_e5m2_x4
+E4M3_X4 = mybir.dt.float8_e4m3fn_x4
+E5M2_X4 = mybir.dt.float8_e5m2_x4
 
 P = 128
 W = 9
-PADW = 4
-HW = 72
+CENTRE = 4
 HALF = 36
-ROW = 128 * HW
-BASE = 12
-COL = 512
+ROW = 128 * 2 * HALF
+COL = 128 * 4
+LEAD = 12
+MAX_QUANT = 4096
+ORDER = (3, 4, 5, 2, 6, 1, 7, 0, 8)
 FLOPS = 2 * 61 * 512 * 512 * 256
 
 
-def span(i):
-    d = i - PADW
+def used_columns(i):
+    d = i - CENTRE
     return d, max(0, -d), W - max(0, d)
 
 
 def tile_scatterhorizontal_kernel(tc, x0, x1, x2, x3, x4, x5, x6, x7, x8, weights, bias, grad_out, out):
     nc = tc.nc
     xs = [x0, x1, x2, x3, x4, x5, x6, x7, x8]
+
+    units = [(grad_out, 0, 0, W), (grad_out, 256, 0, W)]
+    for i in ORDER:
+        d, lo, hi = used_columns(i)
+        units.append((xs[i], 0, lo, hi))
+    n_units = len(units)
+    first_x = 2
+    last = n_units - 1
+
     with ExitStack() as ctx:
         keep = ctx.enter_context(tc.tile_pool(name="keep", bufs=1))
         mid = ctx.enter_context(tc.tile_pool(name="mid", bufs=2))
-        psum_a = ctx.enter_context(tc.psum_pool(name="psum_a", bufs=4))
-        psum_t = ctx.enter_context(tc.psum_pool(name="psum_t", bufs=4))
+        psum_sums = ctx.enter_context(tc.psum_pool(name="psum_sums", bufs=4))
+        psum_back = ctx.enter_context(tc.psum_pool(name="psum_back", bufs=4))
         ctx.enter_context(tc.manual_schedule())
 
         ident = keep.tile([P, P], F32, name="ident")
         make_identity(nc, ident[:])
-        raws = []
-        bts = []
-        qs = []
-        xcs = []
-        xss = []
-        for j in range(3):
-            cols = W if j < 2 else W - 1
-            raw_t = keep.tile([P, BASE + HALF + ROW], BF16, name="raw%d" % j)
-            bt_t = keep.tile([P, cols * COL + 16], BF16, name="bt%d" % j)
-            q_t = keep.tile([P, 2 * cols * COL], BF16, name="q%d" % j, align_bytes=64)
-            xc_t = keep.tile([P, 2 * cols * P], U32, name="xc%d" % j, align_bytes=64)
-            xs_t = keep.tile([P, 2 * cols * P], U8, name="xs%d" % j, align_bytes=64)
-            nc.vector.memset(raw_t[:, 0:16], 0.0)
-            nc.vector.memset(raw_t[:, BASE + ROW - 12:BASE + ROW + HALF], 0.0)
-            raws.append(raw_t)
-            bts.append(bt_t)
-            qs.append(q_t)
-            xcs.append(xc_t)
-            xss.append(xs_t)
-        gc = keep.tile([P, W, 512], U32, name="gc", align_bytes=64)
-        gs = keep.tile([P, W, 512], U8, name="gs", align_bytes=64)
-        osts = []
-        for j in range(7):
-            ost_t = keep.tile([P, 4, 256], F32, name="ost%d" % j)
-            osts.append(ost_t)
 
-        units = [(grad_out, 0, 0, W), (grad_out, 256, 0, W)]
-        order = [3, 4, 5, 2, 6, 1, 7, 0, 8]
-        for i in order:
-            d, lo, hi = span(i)
-            units.append((xs[i], 0, lo, hi))
-        n_units = len(units)
+        raws = []
+        for j in range(4):
+            raw_t = keep.tile([P, LEAD + HALF + ROW], BF16, name="raw%d" % j)
+            nc.vector.memset(raw_t[:, 0:16], 0.0)
+            nc.vector.memset(raw_t[:, LEAD + ROW - 12:LEAD + ROW + HALF], 0.0)
+            raws.append(raw_t)
+        moves = []
+        pairs = []
+        for j in range(2):
+            move_t = keep.tile([P, W * COL + 16], BF16, name="move%d" % j)
+            pair_t = keep.tile([P, 2 * W * COL], BF16, name="pair%d" % j, align_bytes=64)
+            moves.append(move_t)
+            pairs.append(pair_t)
+        x_codes = []
+        x_scales = []
+        for j in range(3):
+            codes_t = keep.tile([P, 2 * W * P], U32, name="x_codes%d" % j, align_bytes=64)
+            scales_t = keep.tile([P, 2 * W * P], U8, name="x_scales%d" % j, align_bytes=64)
+            x_codes.append(codes_t)
+            x_scales.append(scales_t)
+        g_codes = keep.tile([P, W, 512], U32, name="g_codes", align_bytes=64)
+        g_scales = keep.tile([P, W, 512], U8, name="g_scales", align_bytes=64)
+        results = []
+        for j in range(7):
+            result_t = keep.tile([P, 4, 256], F32, name="result%d" % j)
+            results.append(result_t)
 
         def load(u):
-            src, cb = units[u][0], units[u][1]
-            raw = raws[u % 3]
+            src, first_channel = units[u][0], units[u][1]
+            raw = raws[u % 4]
             flat = src.rearrange("b k h w -> b (k h w)")
-            e0 = cb * HW
-            o0 = (cb + 128) * HW
-            nc.sync.dma_start(out=raw[0:P:2, BASE + HALF:BASE + HALF + ROW], in_=flat[:, e0:e0 + ROW])
-            nc.sync.dma_start(out=raw[1:P:2, BASE:BASE + ROW], in_=flat[:, o0:o0 + ROW])
-            nc.sync.dma_start(out=raw[0:P:2, BASE + 1:BASE + HALF], in_=flat[:, e0 + ROW - HALF:e0 + ROW - 1])
+            even = first_channel * 2 * HALF
+            odd = even + ROW
+            nc.sync.dma_start(out=raw[0:P:2, LEAD + HALF:LEAD + HALF + ROW], in_=flat[:, even:even + ROW])
+            nc.sync.dma_start(out=raw[1:P:2, LEAD:LEAD + ROW], in_=flat[:, odd:odd + ROW])
+            nc.sync.dma_start(out=raw[0:P:2, LEAD + 1:LEAD + HALF], in_=flat[:, even + ROW - HALF:even + ROW - 1])
 
         def regroup(u):
             lo, hi = units[u][2], units[u][3]
             n = hi - lo
-            raw = raws[u % 3]
-            bt = bts[u % 3]
-            q = qs[u % 3]
-            a_view = raw[:, BASE + HALF:BASE + HALF + ROW].rearrange("p (k g t w) -> p g k t w", g=2, t=4, w=W)
-            b_view = raw[:, BASE:BASE + ROW].rearrange("p (k g t w) -> p g k t w", g=2, t=4, w=W)
-            tail = raw[:, BASE + ROW:BASE + ROW + HALF].rearrange("p (t w) -> p t w", w=W)
+            raw = raws[u % 4]
+            move = moves[u % 2]
+            pair = pairs[u % 2]
+            stay_view = raw[:, LEAD + HALF:LEAD + HALF + ROW].rearrange("p (k g t w) -> p g k t w", g=2, t=4, w=W)
+            move_view = raw[:, LEAD:LEAD + ROW].rearrange("p (k g t w) -> p g k t w", g=2, t=4, w=W)
             parts = (n + 3) // 4
             cuts = [(n * j) // parts for j in range(parts + 1)]
             for j in range(parts):
-                e0, e1 = cuts[j], cuts[j + 1]
+                c0, c1 = cuts[j], cuts[j + 1]
                 nc.vector.tensor_copy(
-                    out=q[:, e0 * COL:e1 * COL].rearrange("p (c k t) -> p k t c", k=128, t=4),
-                    in_=a_view[:, 0, :, :, lo + e0:lo + e1],
+                    out=pair[:, c0 * COL:c1 * COL].rearrange("p (c k t) -> p k t c", k=128, t=4),
+                    in_=stay_view[:, 0, :, :, lo + c0:lo + c1],
                 )
                 nc.scalar.copy(
-                    out=bt[:, e0 * COL:e1 * COL].rearrange("p (c k t) -> p k t c", k=128, t=4),
-                    in_=b_view[:, 0, :, :, lo + e0:lo + e1],
+                    out=move[:, c0 * COL:c1 * COL].rearrange("p (c k t) -> p k t c", k=128, t=4),
+                    in_=move_view[:, 0, :, :, lo + c0:lo + c1],
                 )
-            nc.scalar.copy(out=bt[:, n * COL:n * COL + 4], in_=tail[:, :, hi - 1])
-            nc.vector.tensor_copy(out=q[:, n * COL:2 * n * COL], in_=q[:, 0:n * COL])
-            nc.scalar.dma_start(out=q[1:P:2, 0:n * COL], in_=bt[0:P:2, 4:n * COL + 4])
-            nc.scalar.dma_start(out=q[0:P:2, n * COL:2 * n * COL], in_=bt[1:P:2, 0:n * COL])
+            end_view = raw[:, LEAD + ROW:LEAD + ROW + HALF].rearrange("p (t w) -> p t w", w=W)
+            nc.scalar.copy(out=move[:, n * COL:n * COL + 4], in_=end_view[:, :, hi - 1])
+            nc.vector.tensor_copy(out=pair[:, n * COL:2 * n * COL], in_=pair[:, 0:n * COL])
+            nc.scalar.dma_start(out=pair[1:P:2, 0:n * COL], in_=move[0:P:2, 4:n * COL + 4])
+            nc.scalar.dma_start(out=pair[0:P:2, n * COL:2 * n * COL], in_=move[1:P:2, 0:n * COL])
 
         def quantise(u):
             n = units[u][3] - units[u][2]
-            q = qs[u % 3]
-            if u < 2:
+            pair = pairs[u % 2]
+            if u < first_x:
                 for s in range(2):
                     for c in range(n):
                         f = (s * n + c) * COL
                         w0 = 256 * u + 128 * s
                         nc.vector.quantize_mx(
-                            out=gc[:, c, w0:w0 + 128].bitcast(E5X4),
-                            scales=gs[:, c, w0:w0 + 128],
-                            in_=q[:, f:f + COL],
+                            out=g_codes[:, c, w0:w0 + 128].bitcast(E5M2_X4),
+                            scales=g_scales[:, c, w0:w0 + 128],
+                            in_=pair[:, f:f + COL],
                         )
-                return
-            f = 0
-            while f < 2 * n * COL:
-                width = 4096
-                while f + width > 2 * n * COL:
-                    width = width // 2
-                nc.vector.quantize_mx(
-                    out=xcs[u % 3][:, f // 4:(f + width) // 4].bitcast(E4X4),
-                    scales=xss[u % 3][:, f // 4:(f + width) // 4],
-                    in_=q[:, f:f + width],
-                )
-                f += width
+            else:
+                f = 0
+                while f < 2 * n * COL:
+                    width = MAX_QUANT
+                    while f + width > 2 * n * COL:
+                        width = width // 2
+                    nc.vector.quantize_mx(
+                        out=x_codes[u % 3][:, f // 4:(f + width) // 4].bitcast(E4M3_X4),
+                        scales=x_scales[u % 3][:, f // 4:(f + width) // 4],
+                        in_=pair[:, f:f + width],
+                    )
+                    f += width
 
-        accs = {}
-        t1s = {}
-        pts = {}
+        sums = {}
+        copies = {}
+        backs = {}
 
-        def matmuls(u):
+        def multiply(u):
             lo, hi = units[u][2], units[u][3]
             n = hi - lo
-            d = order[u - 2] - PADW
+            d = ORDER[u - first_x] - CENTRE
             for s in range(2):
-                acc = psum_a.tile([P, 512], F32, tag="acc")
-                accs[(u, s)] = acc
+                acc = psum_sums.tile([P, 512], F32, tag="acc")
+                sums[(u, s)] = acc
                 for c in range(n):
                     w0 = (s * n + c) * P
                     nc.tensor.matmul_mx(
                         out=acc[:],
-                        lhsT=xcs[u % 3][:, w0:w0 + P].bitcast(E4X4),
-                        lhsT_scale=xss[u % 3][:, w0:w0 + P],
-                        rhs=gc[:, lo + c + d, :].bitcast(E5X4),
-                        rhs_scale=gs[:, lo + c + d, :],
+                        lhsT=x_codes[u % 3][:, w0:w0 + P].bitcast(E4M3_X4),
+                        lhsT_scale=x_scales[u % 3][:, w0:w0 + P],
+                        rhs=g_codes[:, lo + c + d, :].bitcast(E5M2_X4),
+                        rhs_scale=g_scales[:, lo + c + d, :],
                         start=(c == 0),
                         stop=(c == n - 1),
                     )
 
-        def evac1(u):
-            t1 = mid.tile([P, 2, 512], F32, tag="t1")
-            t1s[u] = t1
-            nc.scalar.copy(out=t1[:, 0, :], in_=accs[(u, 0)][:])
-            if u == n_units - 1:
-                nc.vector.tensor_copy(out=t1[:, 1, :], in_=accs[(u, 1)][:])
-            else:
-                nc.scalar.copy(out=t1[:, 1, :], in_=accs[(u, 1)][:])
+        def second_engine(u):
+            return nc.vector.tensor_copy if u == last else nc.scalar.copy
 
-        def transposes(u):
+        def copy_out(u):
+            copy_t = mid.tile([P, 2, 512], F32, tag="copy")
+            copies[u] = copy_t
+            nc.scalar.copy(out=copy_t[:, 0, :], in_=sums[(u, 0)][:])
+            second_engine(u)(out=copy_t[:, 1, :], in_=sums[(u, 1)][:])
+
+        def transpose_back(u):
             for h in range(2):
-                pt = psum_t.tile([P, 2, 2, P], F32, tag="pt")
-                pts[(u, h)] = pt
-                for o2 in range(2):
+                back = psum_back.tile([P, 2, 2, P], F32, tag="back")
+                backs[(u, h)] = back
+                for j in range(2):
                     for s in range(2):
-                        ot = 2 * h + o2
-                        nc.tensor.transpose(pt[:, o2, s, :], t1s[u][:, s, P * ot:P * ot + P], ident[:])
+                        o0 = P * (2 * h + j)
+                        nc.tensor.transpose(back[:, j, s, :], copies[u][:, s, o0:o0 + P], ident[:])
 
-        def evac2(u):
-            ost = osts[(u - 2) % 7]
-            nc.scalar.copy(out=ost[:, 0:2, :], in_=pts[(u, 0)][:].rearrange("p a s k -> p a (s k)"))
-            if u == n_units - 1:
-                nc.vector.tensor_copy(out=ost[:, 2:4, :], in_=pts[(u, 1)][:].rearrange("p a s k -> p a (s k)"))
+        def collect(u):
+            result = results[(u - first_x) % 7]
+            nc.scalar.copy(out=result[:, 0:2, :], in_=backs[(u, 0)][:].rearrange("p j s k -> p j (s k)"))
+            second_engine(u)(out=result[:, 2:4, :], in_=backs[(u, 1)][:].rearrange("p j s k -> p j (s k)"))
+
+        def store(u, queue):
+            dst = out[ORDER[u - first_x]].rearrange("(j o) k -> o j k", o=P)
+            result = results[(u - first_x) % 7]
+            if u == last:
+                nc.scalar.dma_start(out=dst[:, 0:2, :], in_=result[:, 0:2, :])
+                nc.sync.dma_start(out=dst[:, 2:4, :], in_=result[:, 2:4, :])
             else:
-                nc.scalar.copy(out=ost[:, 2:4, :], in_=pts[(u, 1)][:].rearrange("p a s k -> p a (s k)"))
+                queue.dma_start(out=dst, in_=result[:])
 
-        def store(u):
-            dst = out[order[u - 2]].rearrange("(t o) k -> o t k", o=P)
-            ost = osts[(u - 2) % 7]
-            if u == n_units - 1:
-                nc.scalar.dma_start(out=dst[:, 0:2, :], in_=ost[:, 0:2, :])
-                nc.sync.dma_start(out=dst[:, 2:4, :], in_=ost[:, 2:4, :])
-            elif u <= 4:
-                nc.sync.dma_start(out=dst, in_=ost[:])
-            else:
-                nc.scalar.dma_start(out=dst, in_=ost[:])
-
-        z_next = 0
-        waiting = []
-        for t in range(n_units + 6):
+        ready = []
+        for t in range(n_units + 3):
             if t == 0:
                 load(0)
                 load(1)
-            if t + 2 < n_units:
-                load(t + 2)
+                load(2)
+            if t + 3 < n_units:
+                load(t + 3)
             if t < n_units:
                 regroup(t)
-            z_end = t - 1 if t >= 9 else t - 2
-            while z_next <= min(z_end, n_units - 1):
-                quantise(z_next)
-                if z_next >= 2:
-                    matmuls(z_next)
-                z_next += 1
-            e_unit = t - 3
-            if 2 <= e_unit < n_units:
-                evac1(e_unit)
-                transposes(e_unit)
-            f_unit = t - 4
-            if 2 <= f_unit < n_units:
-                evac2(f_unit)
-                waiting.append(f_unit)
-            if t >= n_units - 1 or t == n_units - 3:
-                for u in waiting:
-                    store(u)
-                waiting = []
+            if 0 <= t - 1 < n_units:
+                quantise(t - 1)
+                if t - 1 >= first_x:
+                    multiply(t - 1)
+            if first_x <= t - 2 < n_units:
+                copy_out(t - 2)
+                transpose_back(t - 2)
+            if first_x <= t - 3 < n_units:
+                collect(t - 3)
+                ready.append(t - 3)
+            if t + 3 == last or t >= last:
+                for u in ready:
+                    store(u, nc.sync if t + 3 == last else nc.scalar)
+                ready = []

@@ -17,6 +17,7 @@ HALF = 36
 ROW = 128 * 2 * HALF
 COL = 128 * 4
 LEAD = 12
+EDGE = HALF + 2
 MAX_QUANT = 4096
 ORDER = (3, 4, 5, 2, 6, 1, 7, 0, 8)
 FLOPS = 2 * 61 * 512 * 512 * 256
@@ -52,9 +53,13 @@ def tile_scatterhorizontal_kernel(tc, x0, x1, x2, x3, x4, x5, x6, x7, x8, weight
         raws = []
         for j in range(4):
             raw_t = keep.tile([P, LEAD + HALF + ROW], BF16, name="raw%d" % j)
-            nc.vector.memset(raw_t[:, 0:16], 0.0)
             nc.vector.memset(raw_t[:, LEAD + ROW - 12:LEAD + ROW + HALF], 0.0)
             raws.append(raw_t)
+        edges = []
+        for j in range(4):
+            edge_t = keep.tile([P, EDGE], BF16, name="edge%d" % j)
+            nc.vector.memset(edge_t[:], 0.0)
+            edges.append(edge_t)
         moves = []
         pairs = []
         for j in range(2):
@@ -84,7 +89,9 @@ def tile_scatterhorizontal_kernel(tc, x0, x1, x2, x3, x4, x5, x6, x7, x8, weight
             odd = even + ROW
             nc.sync.dma_start(out=raw[0:P:2, LEAD + HALF:LEAD + HALF + ROW], in_=flat[:, even:even + ROW])
             nc.sync.dma_start(out=raw[1:P:2, LEAD:LEAD + ROW], in_=flat[:, odd:odd + ROW])
-            nc.sync.dma_start(out=raw[0:P:2, LEAD + 1:LEAD + HALF], in_=flat[:, even + ROW - HALF:even + ROW - 1])
+            edge = edges[u % 4]
+            nc.sync.dma_start(out=edge[1:P:2, 0:EDGE], in_=flat[:, odd - 1:odd - 1 + EDGE])
+            nc.sync.dma_start(out=edge[0:P:2, 2:EDGE], in_=flat[:, even + ROW - HALF:even + ROW])
 
         def regroup(u):
             lo, hi = units[u][2], units[u][3]
@@ -103,9 +110,13 @@ def tile_scatterhorizontal_kernel(tc, x0, x1, x2, x3, x4, x5, x6, x7, x8, weight
                     in_=stay_view[:, 0, :, :, lo + c0:lo + c1],
                 )
                 nc.scalar.copy(
-                    out=move[:, c0 * COL:c1 * COL].rearrange("p (c k t) -> p k t c", k=128, t=4),
-                    in_=move_view[:, 0, :, :, lo + c0:lo + c1],
+                    out=move[:, c0 * COL:c1 * COL].rearrange("p (c k t) -> p k t c", k=128, t=4)[:, 1:128, :, :],
+                    in_=move_view[:, 0, 1:128, :, lo + c0:lo + c1],
                 )
+            nc.scalar.copy(
+                out=move[:, 0:n * COL].rearrange("p (c k t) -> p k t c", k=128, t=4)[:, 0, :, :],
+                in_=edges[u % 4][:, 1:1 + HALF].rearrange("p (t w) -> p t w", w=W)[:, :, lo:hi],
+            )
             end_view = raw[:, LEAD + ROW:LEAD + ROW + HALF].rearrange("p (t w) -> p t w", w=W)
             nc.scalar.copy(out=move[:, n * COL:n * COL + 4], in_=end_view[:, :, hi - 1])
             nc.vector.tensor_copy(out=pair[:, n * COL:2 * n * COL], in_=pair[:, 0:n * COL])

@@ -178,8 +178,11 @@ def tile_scatterhorizontal_kernel(tc, x0, x1, x2, x3, x4, x5, x6, x7, x8, weight
         def copy_out(u):
             copy_t = mid.tile([P, 2, 512], F32, tag="copy")
             copies[u] = copy_t
-            nc.scalar.copy(out=copy_t[:, 0, :], in_=sums[(u, 0)][:])
-            second_engine(u)(out=copy_t[:, 1, :], in_=sums[(u, 1)][:])
+            for s, engine_copy in ((0, nc.scalar.copy), (1, second_engine(u))):
+                engine_copy(
+                    out=copy_t[:, s, :].rearrange("p (j m) -> p j m", j=4),
+                    in_=sums[(u, s)][:].rearrange("p (m j) -> p j m", j=4),
+                )
 
         def transpose_back(u):
             for h in range(2):
@@ -196,7 +199,7 @@ def tile_scatterhorizontal_kernel(tc, x0, x1, x2, x3, x4, x5, x6, x7, x8, weight
             second_engine(u)(out=result[:, 2:4, :], in_=backs[(u, 1)][:].rearrange("p j s k -> p j (s k)"))
 
         def store(u, queue):
-            dst = out[ORDER[u - first_x]].rearrange("(j o) k -> o j k", o=P)
+            dst = out[ORDER[u - first_x]].rearrange("(m j) k -> m j k", j=4)
             result = results[(u - first_x) % 7]
             if u == last:
                 nc.scalar.dma_start(out=dst[:, 0:2, :], in_=result[:, 0:2, :])

@@ -81,14 +81,24 @@ def tile_scatterhorizontal_kernel(tc, x0, x1, x2, x3, x4, x5, x6, x7, x8, weight
             result_t = keep.tile([P, 4, 256], F32, name="result%d" % j)
             results.append(result_t)
 
+        def channel_cuts(u):
+            return 2 if u in (0, last) else 1
+
         def load(u):
             src, first_channel = units[u][0], units[u][1]
             raw = raws[u % 4]
             flat = src.rearrange("b k h w -> b (k h w)")
             even = first_channel * 2 * HALF
             odd = even + ROW
-            nc.sync.dma_start(out=raw[0:P:2, LEAD + HALF:LEAD + HALF + ROW], in_=flat[:, even:even + ROW])
-            nc.sync.dma_start(out=raw[1:P:2, LEAD:LEAD + ROW], in_=flat[:, odd:odd + ROW])
+            if channel_cuts(u) == 2:
+                even_cuts, odd_cuts = (0, ROW // 2, ROW), (0, ROW // 2 + 4, ROW)
+            else:
+                even_cuts, odd_cuts = (0, ROW), (0, ROW)
+            for j in range(channel_cuts(u)):
+                a, b = even_cuts[j], even_cuts[j + 1]
+                nc.sync.dma_start(out=raw[0:P:2, LEAD + HALF + a:LEAD + HALF + b], in_=flat[:, even + a:even + b])
+                a, b = odd_cuts[j], odd_cuts[j + 1]
+                nc.sync.dma_start(out=raw[1:P:2, LEAD + a:LEAD + b], in_=flat[:, odd + a:odd + b])
             edge = edges[u % 4]
             nc.sync.dma_start(out=edge[1:P:2, 0:EDGE], in_=flat[:, odd - 1:odd - 1 + EDGE])
             nc.sync.dma_start(out=edge[0:P:2, 2:EDGE], in_=flat[:, even + ROW - HALF:even + ROW])
@@ -103,16 +113,19 @@ def tile_scatterhorizontal_kernel(tc, x0, x1, x2, x3, x4, x5, x6, x7, x8, weight
             move_view = raw[:, LEAD:LEAD + ROW].rearrange("p (k g t w) -> p g k t w", g=2, t=4, w=W)
             parts = (n + 3) // 4
             cuts = [(n * j) // parts for j in range(parts + 1)]
-            for j in range(parts):
-                c0, c1 = cuts[j], cuts[j + 1]
-                nc.vector.tensor_copy(
-                    out=pair[:, c0 * COL:c1 * COL].rearrange("p (c k t) -> p k t c", k=128, t=4),
-                    in_=stay_view[:, 0, :, :, lo + c0:lo + c1],
-                )
-                nc.scalar.copy(
-                    out=move[:, c0 * COL:c1 * COL].rearrange("p (c k t) -> p k t c", k=128, t=4)[:, 1:128, :, :],
-                    in_=move_view[:, 0, 1:128, :, lo + c0:lo + c1],
-                )
+            channels = 128 // channel_cuts(u)
+            for k0 in range(0, 128, channels):
+                k1 = k0 + channels
+                for j in range(parts):
+                    c0, c1 = cuts[j], cuts[j + 1]
+                    nc.vector.tensor_copy(
+                        out=pair[:, c0 * COL:c1 * COL].rearrange("p (c k t) -> p k t c", k=128, t=4)[:, k0:k1, :, :],
+                        in_=stay_view[:, 0, k0:k1, :, lo + c0:lo + c1],
+                    )
+                    nc.scalar.copy(
+                        out=move[:, c0 * COL:c1 * COL].rearrange("p (c k t) -> p k t c", k=128, t=4)[:, max(k0, 1):k1, :, :],
+                        in_=move_view[:, 0, max(k0, 1):k1, :, lo + c0:lo + c1],
+                    )
             nc.scalar.copy(
                 out=move[:, 0:n * COL].rearrange("p (c k t) -> p k t c", k=128, t=4)[:, 0, :, :],
                 in_=edges[u % 4][:, 1:1 + HALF].rearrange("p (t w) -> p t w", w=W)[:, :, lo:hi],

from contextlib import ExitStack

import concourse.mybir as mybir
from concourse.masks import make_identity

BF16 = mybir.dt.bfloat16
F32 = mybir.dt.float32
U32 = mybir.dt.uint32
U8 = mybir.dt.uint8
E4M3_X4 = mybir.dt.float8_e4m3fn_x4
E5M2_X4 = mybir.dt.float8_e5m2_x4

P = 128
W = 9
CENTRE = 4
HALF = 36
ROW = 128 * 2 * HALF
COL = 128 * 4
LEAD = 12
EDGE = HALF + 2
MAX_QUANT = 4096
ORDER = (3, 4, 5, 2, 6, 1, 7, 0, 8)
FLOPS = 2 * 61 * 512 * 512 * 256


def used_columns(i):
    d = i - CENTRE
    return d, max(0, -d), W - max(0, d)


def tile_scatterhorizontal_kernel(tc, x0, x1, x2, x3, x4, x5, x6, x7, x8, weights, bias, grad_out, out):
    nc = tc.nc
    xs = [x0, x1, x2, x3, x4, x5, x6, x7, x8]

    units = [(grad_out, 0, 0, W), (grad_out, 256, 0, W)]
    for i in ORDER:
        d, lo, hi = used_columns(i)
        units.append((xs[i], 0, lo, hi))
    n_units = len(units)
    first_x = 2
    last = n_units - 1

    with ExitStack() as ctx:
        keep = ctx.enter_context(tc.tile_pool(name="keep", bufs=1))
        mid = ctx.enter_context(tc.tile_pool(name="mid", bufs=2))
        psum_sums = ctx.enter_context(tc.psum_pool(name="psum_sums", bufs=4))
        psum_back = ctx.enter_context(tc.psum_pool(name="psum_back", bufs=4))
        ctx.enter_context(tc.manual_schedule())

        ident = keep.tile([P, P], F32, name="ident")
        make_identity(nc, ident[:])

        raws = []
        for j in range(4):
            raw_t = keep.tile([P, LEAD + HALF + ROW], BF16, name="raw%d" % j)
            nc.vector.memset(raw_t[:, LEAD + ROW - 12:LEAD + ROW + HALF], 0.0)
            raws.append(raw_t)
        edges = []
        for j in range(4):
            edge_t = keep.tile([P, EDGE], BF16, name="edge%d" % j)
            nc.vector.memset(edge_t[:], 0.0)
            edges.append(edge_t)
        moves = []
        pairs = []
        for j in range(2):
            move_t = keep.tile([P, W * COL + 16], BF16, name="move%d" % j)
            pair_t = keep.tile([P, 2 * W * COL], BF16, name="pair%d" % j, align_bytes=64)
            moves.append(move_t)
            pairs.append(pair_t)
        x_codes = []
        x_scales = []
        for j in range(3):
            codes_t = keep.tile([P, 2 * W * P], U32, name="x_codes%d" % j, align_bytes=64)
            scales_t = keep.tile([P, 2 * W * P], U8, name="x_scales%d" % j, align_bytes=64)
            x_codes.append(codes_t)
            x_scales.append(scales_t)
        g_codes = keep.tile([P, W, 512], U32, name="g_codes", align_bytes=64)
        g_scales = keep.tile([P, W, 512], U8, name="g_scales", align_bytes=64)
        results = []
        for j in range(7):
            result_t = keep.tile([P, 4, 256], F32, name="result%d" % j)
            results.append(result_t)

        def channel_cuts(u):
            return 2 if u in (0, last) else 1

        def load(u):
            src, first_channel = units[u][0], units[u][1]
            raw = raws[u % 4]
            flat = src.rearrange("b k h w -> b (k h w)")
            even = first_channel * 2 * HALF
            odd = even + ROW
            if channel_cuts(u) == 2:
                even_cuts, odd_cuts = (0, ROW // 2, ROW), (0, ROW // 2 + 4, ROW)
            else:
                even_cuts, odd_cuts = (0, ROW), (0, ROW)
            for j in range(channel_cuts(u)):
                a, b = even_cuts[j], even_cuts[j + 1]
                nc.sync.dma_start(out=raw[0:P:2, LEAD + HALF + a:LEAD + HALF + b], in_=flat[:, even + a:even + b])
                a, b = odd_cuts[j], odd_cuts[j + 1]
                nc.sync.dma_start(out=raw[1:P:2, LEAD + a:LEAD + b], in_=flat[:, odd + a:odd + b])
            edge = edges[u % 4]
            nc.sync.dma_start(out=edge[1:P:2, 0:EDGE], in_=flat[:, odd - 1:odd - 1 + EDGE])
            nc.sync.dma_start(out=edge[0:P:2, 2:EDGE], in_=flat[:, even + ROW - HALF:even + ROW])

        def regroup(u):
            lo, hi = units[u][2], units[u][3]
            n = hi - lo
            raw = raws[u % 4]
            move = moves[u % 2]
            pair = pairs[u % 2]
            stay_view = raw[:, LEAD + HALF:LEAD + HALF + ROW].rearrange("p (k g t w) -> p g k t w", g=2, t=4, w=W)
            move_view = raw[:, LEAD:LEAD + ROW].rearrange("p (k g t w) -> p g k t w", g=2, t=4, w=W)
            parts = (n + 3) // 4
            cuts = [(n * j) // parts for j in range(parts + 1)]
            channels = 128 // channel_cuts(u)
            for k0 in range(0, 128, channels):
                k1 = k0 + channels
                for j in range(parts):
                    c0, c1 = cuts[j], cuts[j + 1]
                    nc.vector.tensor_copy(
                        out=pair[:, c0 * COL:c1 * COL].rearrange("p (c k t) -> p k t c", k=128, t=4)[:, k0:k1, :, :],
                        in_=stay_view[:, 0, k0:k1, :, lo + c0:lo + c1],
                    )
                    nc.scalar.copy(
                        out=move[:, c0 * COL:c1 * COL].rearrange("p (c k t) -> p k t c", k=128, t=4)[:, max(k0, 1):k1, :, :],
                        in_=move_view[:, 0, max(k0, 1):k1, :, lo + c0:lo + c1],
                    )
            nc.scalar.copy(
                out=move[:, 0:n * COL].rearrange("p (c k t) -> p k t c", k=128, t=4)[:, 0, :, :],
                in_=edges[u % 4][:, 1:1 + HALF].rearrange("p (t w) -> p t w", w=W)[:, :, lo:hi],
            )
            end_view = raw[:, LEAD + ROW:LEAD + ROW + HALF].rearrange("p (t w) -> p t w", w=W)
            nc.scalar.copy(out=move[:, n * COL:n * COL + 4], in_=end_view[:, :, hi - 1])
            nc.vector.tensor_copy(out=pair[:, n * COL:2 * n * COL], in_=pair[:, 0:n * COL])
            nc.scalar.dma_start(out=pair[1:P:2, 0:n * COL], in_=move[0:P:2, 4:n * COL + 4])
            nc.scalar.dma_start(out=pair[0:P:2, n * COL:2 * n * COL], in_=move[1:P:2, 0:n * COL])

        def quantise(u):
            n = units[u][3] - units[u][2]
            pair = pairs[u % 2]
            if u < first_x:
                for s in range(2):
                    for c in range(n):
                        f = (s * n + c) * COL
                        w0 = 256 * u + 128 * s
                        nc.vector.quantize_mx(
                            out=g_codes[:, c, w0:w0 + 128].bitcast(E5M2_X4),
                            scales=g_scales[:, c, w0:w0 + 128],
                            in_=pair[:, f:f + COL],
                        )
            else:
                f = 0
                while f < 2 * n * COL:
                    width = MAX_QUANT
                    while f + width > 2 * n * COL:
                        width = width // 2
                    nc.vector.quantize_mx(
                        out=x_codes[u % 3][:, f // 4:(f + width) // 4].bitcast(E4M3_X4),
                        scales=x_scales[u % 3][:, f // 4:(f + width) // 4],
                        in_=pair[:, f:f + width],
                    )
                    f += width

        sums = {}
        copies = {}
        backs = {}

        def multiply(u):
            lo, hi = units[u][2], units[u][3]
            n = hi - lo
            d = ORDER[u - first_x] - CENTRE
            for s in range(2):
                acc = psum_sums.tile([P, 512], F32, tag="acc")
                sums[(u, s)] = acc
                for c in range(n):
                    w0 = (s * n + c) * P
                    nc.tensor.matmul_mx(
                        out=acc[:],
                        lhsT=x_codes[u % 3][:, w0:w0 + P].bitcast(E4M3_X4),
                        lhsT_scale=x_scales[u % 3][:, w0:w0 + P],
                        rhs=g_codes[:, lo + c + d, :].bitcast(E5M2_X4),
                        rhs_scale=g_scales[:, lo + c + d, :],
                        start=(c == 0),
                        stop=(c == n - 1),
                    )

        def second_engine(u):
            return nc.vector.tensor_copy if u == last else nc.scalar.copy

        def copy_out(u):
            copy_t = mid.tile([P, 2, 512], F32, tag="copy")
            copies[u] = copy_t
            for s, engine_copy in ((0, nc.scalar.copy), (1, second_engine(u))):
                engine_copy(
                    out=copy_t[:, s, :].rearrange("p (j m) -> p j m", j=4),
                    in_=sums[(u, s)][:].rearrange("p (m j) -> p j m", j=4),
                )

        def transpose_back(u):
            for h in range(2):
                back = psum_back.tile([P, 2, 2, P], F32, tag="back")
                backs[(u, h)] = back
                for j in range(2):
                    for s in range(2):
                        o0 = P * (2 * h + j)
                        nc.tensor.transpose(back[:, j, s, :], copies[u][:, s, o0:o0 + P], ident[:])

        def collect(u):
            result = results[(u - first_x) % 7]
            nc.scalar.copy(out=result[:, 0:2, :], in_=backs[(u, 0)][:].rearrange("p j s k -> p j (s k)"))
            second_engine(u)(out=result[:, 2:4, :], in_=backs[(u, 1)][:].rearrange("p j s k -> p j (s k)"))

        def store(u, queue):
            dst = out[ORDER[u - first_x]].rearrange("(m j) k -> m j k", j=4)
            result = results[(u - first_x) % 7]
            if u == last:
                nc.scalar.dma_start(out=dst[:, 0:2, :], in_=result[:, 0:2, :])
                nc.sync.dma_start(out=dst[:, 2:4, :], in_=result[:, 2:4, :])
            else:
                queue.dma_start(out=dst, in_=result[:])

        ready = []
        for t in range(n_units + 3):
            if t == 0:
                load(0)
                load(1)
                load(2)
            if t + 3 < n_units:
                load(t + 3)
            if t < n_units:
                regroup(t)
            if 0 <= t - 1 < n_units:
                quantise(t - 1)
                if t - 1 >= first_x:
                    multiply(t - 1)
            if first_x <= t - 2 < n_units:
                copy_out(t - 2)
                transpose_back(t - 2)
            if first_x <= t - 3 < n_units:
                collect(t - 3)
                ready.append(t - 3)
            if t + 3 == last or t >= last:
                for u in ready:
                    store(u, nc.sync if t + 3 == last else nc.scalar)
                ready = []
